import numpy as np
import ml_dtypes


def mxq(x, axis, fmt="e4m3"):
    dtype, down = {"e4m3": (ml_dtypes.float8_e4m3fn, 7), "e5m2": (ml_dtypes.float8_e5m2, 14)}[fmt]
    v = np.moveaxis(np.asarray(x, np.float32).astype(ml_dtypes.bfloat16).astype(np.float64), axis, -1)
    blocks = v.reshape(v.shape[:-1] + (-1, 32))
    amax = np.abs(blocks).max(-1, keepdims=True)
    byte = np.maximum(np.where(amax > 0, np.frexp(amax)[1] - 1 + 127, 0) - down, 1)
    scale = np.exp2(byte - 127.0)
    codes = (blocks / scale).astype(np.float32).astype(dtype).astype(np.float64)
    return np.moveaxis((codes * scale).reshape(v.shape), -1, axis)


WIDE = False


def mx_kscale(k):
    if not WIDE:
        return np.ones(k)
    levels = np.array([10, -10, 5, -5, 0])
    a = np.random.permutation(np.resize(levels, k // 512 * 4)).reshape(k // 512, 4)
    idx = np.arange(k)
    return np.exp2(a[idx // 512, idx % 128 // 32])


BF16 = ml_dtypes.bfloat16


def bf(x):
    return np.asarray(x, np.float32).astype(BF16)


def f64(x):
    return np.asarray(x).astype(np.float64)


M, SP, H, FF, NH = 512, 384, 1024, 2560, 8
EPS = 1.1920929e-07


def rms_norm(x, w):
    var = np.mean(np.square(x), axis=-1, keepdims=True)
    return x * (1.0 / np.sqrt(var + EPS)) * w


def silu(v):
    return v / (1.0 + np.exp(-v))


def setup_inputs():
    s, t = mx_kscale(H), mx_kscale(H)
    return {"attn": bf(np.random.standard_normal((M, H)) * 0.25 * s),
            "x": bf(np.random.standard_normal((M, H))),
            "W_o": bf(np.random.standard_normal((2, H, H)) * 2.0 / np.sqrt(H) / s[None, :, None]),
            "W_gu": bf(np.random.standard_normal((2, H, 2 * FF)) / np.sqrt(H) / t[None, :, None]),
            "ln2": bf((1.0 + 0.1 * np.random.standard_normal((2, H))) * t)}


def reference(attn, x, W_o, W_gu, ln2):
    attn, x, W_o, W_gu, ln2 = f64(attn), f64(x), f64(W_o), f64(W_gu), f64(ln2)
    o0 = mxq(attn[:SP], 1, "e4m3") @ mxq(W_o[0], 0, "e4m3")
    o1 = mxq(attn[SP:], 1, "e4m3") @ mxq(W_o[1], 0, "e4m3")
    x_mid = x + np.concatenate([o0, o1], axis=0)
    h0 = rms_norm(x_mid[:SP], ln2[0])
    h1 = rms_norm(x_mid[SP:], ln2[1])
    gu0 = mxq(h0, 1, "e4m3") @ mxq(W_gu[0], 0, "e4m3")
    gu1 = mxq(h1, 1, "e4m3") @ mxq(W_gu[1], 0, "e4m3")
    gu = np.concatenate([gu0, gu1], axis=0)
    gate, up = np.split(gu, 2, axis=-1)
    return x_mid, silu(gate) * up

@@ -1,0 +1,279 @@
+from contextlib import ExitStack
+
+import concourse.mybir as mybir
+from concourse.masks import make_identity
+
+F32 = mybir.dt.float32
+BF16 = mybir.dt.bfloat16
+U32 = mybir.dt.uint32
+U8 = mybir.dt.uint8
+FP8X4 = mybir.dt.float8_e4m3fn_x4
+ACT = mybir.ActivationFunctionType
+ALU = mybir.AluOpType
+
+P = 128
+PACK = 4
+K_PASS = P * PACK
+ROWS, SPLIT_ROW, H, FF = 512, 384, 1024, 2560
+EPS = 1.1920929e-07
+MODELS = 2
+PASSES = H // K_PASS
+ROW_TILES = ROWS // P
+N_TILE = 512
+QUANT_COLS = 1024
+UNIT = FF // 2
+RUN = 4
+RAW_BUFS = 4
+
+FLOPS = 2 * ROWS * H * H + 2 * ROWS * H * 2 * FF
+
+
+def model_of(row_tile):
+    return 0 if row_tile * P < SPLIT_ROW else 1
+
+
+def n_tiles(width):
+    return [(first, min(N_TILE, width - first)) for first in range(0, width, N_TILE)]
+
+
+def tile_twomodelblockrouted_pb_kernel(tc, attn, x, W_o, W_gu, ln2, x_mid_out, h_mlp_out):
+    nc = tc.nc
+    with ExitStack() as stack:
+        keep = stack.enter_context(tc.tile_pool(name="keep", bufs=1))
+        raw_pool = stack.enter_context(tc.tile_pool(name="raw", bufs=RAW_BUFS))
+        grouped_pool = stack.enter_context(tc.tile_pool(name="grouped", bufs=3))
+        codes_pool = stack.enter_context(tc.tile_pool(name="codes", bufs=2))
+        work = stack.enter_context(tc.tile_pool(name="work", bufs=2))
+        rows_pool = stack.enter_context(tc.tile_pool(name="rows", bufs=ROW_TILES))
+        result_pool = stack.enter_context(tc.tile_pool(name="result", bufs=3))
+        turned_pool = stack.enter_context(tc.psum_pool(name="turned", bufs=2))
+        acc_pool = stack.enter_context(tc.psum_pool(name="acc", bufs=6))
+
+        ident_f32 = keep.tile([P, P], F32)
+        make_identity(nc, ident_f32[:])
+        ident_bf16 = keep.tile([P, P], BF16)
+        make_identity(nc, ident_bf16[:])
+        one = keep.tile([P, 1], F32)
+        nc.vector.memset(one[:], 1.0)
+        warm = keep.tile([P, 1], F32)
+        nc.scalar.sqrt(out=warm[:], in_=one[:])
+
+        attn_sb = keep.tile([P, ROW_TILES, H], BF16)
+        x_sb = keep.tile([P, ROW_TILES, H], BF16)
+        gains = keep.tile([P, MODELS, H], BF16)
+        x_mid = keep.tile([P, ROW_TILES, H], F32)
+        attn_codes = keep.tile([P, ROW_TILES, PASSES * P], U32, align_bytes=64)
+        attn_scales = keep.tile([P, ROW_TILES, PASSES * P], U8, align_bytes=64)
+        h_codes = keep.tile([P, ROW_TILES, PASSES * P], U32, align_bytes=64)
+        h_scales = keep.tile([P, ROW_TILES, PASSES * P], U8, align_bytes=64)
+        wo_codes = keep.tile([P, MODELS, PASSES, H], U32, align_bytes=64)
+        wo_scales = keep.tile([P, MODELS, PASSES, H], U8, align_bytes=64)
+        sum_sq = keep.tile([P, ROW_TILES], F32)
+        variance = keep.tile([P, ROW_TILES], F32)
+        std = keep.tile([P, ROW_TILES], F32)
+        rstd = keep.tile([P, ROW_TILES], F32)
+
+        units = [("o", g, 0, 0, c) for g in range(MODELS) for c in range(PASSES)]
+        groups = [(g, q) for g in range(MODELS) for q in range(FF // UNIT)]
+        units.extend([("gu", g, q, half, c) for g, q in groups for half in range(2) for c in range(PASSES)])
+        stream = {"steps": 0}
+        raw_of, grouped_of, codes_of = {}, {}, {}
+
+        def width_of(i):
+            return H if units[i][0] == "o" else UNIT
+
+        def load(i):
+            kind, g, q, half, c = units[i]
+            raw = raw_pool.tile([P, PACK, UNIT], BF16, name="raw")
+            k_rows = slice(c * K_PASS, (c + 1) * K_PASS)
+            if kind == "o":
+                for u in range(2):
+                    rows = W_o[g, c * K_PASS + u * 2 * P : c * K_PASS + (u + 1) * 2 * P, :]
+                    nc.sync.dma_start(out=raw[:, 2 * u : 2 * u + 2, :H], in_=rows.rearrange("(p e) n -> p e n", e=2))
+            else:
+                first = half * FF + q * UNIT
+                rows = W_gu[g, k_rows, first : first + UNIT]
+                nc.sync.dma_start(out=raw[:], in_=rows.rearrange("(t p) n -> p t n", p=P))
+            raw_of[i] = raw
+
+        def regroup(i):
+            width = width_of(i)
+            grouped = grouped_pool.tile([P, UNIT, PACK], BF16, name="grouped", align_bytes=64)
+            for copy, first, last in ((nc.vector.tensor_copy, 0, width // 2), (nc.scalar.copy, width // 2, width)):
+                copy(
+                    out=grouped[:, first:last, :].rearrange("p (c i) t -> p c t i", i=RUN),
+                    in_=raw_of[i][:, :, first:last].rearrange("p t (c i) -> p c t i", i=RUN),
+                )
+            grouped_of[i] = grouped
+
+        def quantise(i):
+            kind, g, q, half, c = units[i]
+            if kind == "o":
+                codes, scales = wo_codes[:, g, c, :], wo_scales[:, g, c, :]
+            else:
+                if c == 0:
+                    half_codes = codes_pool.tile([P, PASSES, UNIT], U32, name="codes%d" % half, align_bytes=64)
+                    half_scales = codes_pool.tile([P, PASSES, UNIT], U8, name="scales%d" % half, align_bytes=64)
+                    codes_of[(g, q, half)] = (half_codes, half_scales)
+                codes, scales = codes_of[(g, q, half)][0][:, c, :], codes_of[(g, q, half)][1][:, c, :]
+            for first in range(0, width_of(i), QUANT_COLS):
+                last = min(first + QUANT_COLS, width_of(i))
+                nc.vector.quantize_mx(
+                    out=codes[:, first:last].bitcast(FP8X4),
+                    scales=scales[:, first:last],
+                    in_=grouped_of[i][:, first:last, :].rearrange("p n t -> p (n t)"),
+                )
+
+        def advance():
+            step = stream["steps"]
+            stream["steps"] = step + 1
+            if step < len(units):
+                regroup(step)
+            if 1 <= step <= len(units):
+                quantise(step - 1)
+            if step + RAW_BUFS < len(units):
+                load(step + RAW_BUFS)
+
+        def advance_until_quantised(unit):
+            while stream["steps"] < units.index(unit) + 2:
+                advance()
+
+        def quantise_rows(grouped, codes, scales, rt):
+            nc.vector.quantize_mx(out=codes[:, rt, :].bitcast(FP8X4), scales=scales[:, rt, :], in_=grouped[:])
+
+        def product(rows_codes, rows_scales, rt, w_codes, w_scales, first, width):
+            acc = acc_pool.tile([P, N_TILE], F32, name="acc")
+            for c in range(PASSES):
+                nc.tensor.matmul_mx(
+                    out=acc[:, :width],
+                    lhsT=rows_codes[:, rt, c * P : (c + 1) * P].bitcast(FP8X4),
+                    lhsT_scale=rows_scales[:, rt, c * P : (c + 1) * P],
+                    rhs=w_codes[:, c, first : first + width].bitcast(FP8X4),
+                    rhs_scale=w_scales[:, c, first : first + width],
+                    start=(c == 0),
+                    stop=(c == PASSES - 1),
+                )
+            return acc
+
+        def turn_attn(rt):
+            words = attn_sb[:, rt, :].bitcast(F32)
+            turned = turned_pool.tile([P, PASSES * 2, P], F32, name="turned")
+            for plane in range(PASSES * 2):
+                nc.tensor.transpose(turned[:, plane, :], words[:, plane * P : (plane + 1) * P], ident_f32[:])
+            grouped = rows_pool.tile([P, PASSES * P * PACK], BF16, name="rows_grouped", align_bytes=64)
+            nc.scalar.copy(
+                out=grouped[:].bitcast(F32).rearrange("p (c r u) -> p c r u", c=PASSES, u=2),
+                in_=turned[:].rearrange("p (c u) r -> p c r u", u=2),
+            )
+            return grouped
+
+        def first_product(rt):
+            g = model_of(rt)
+            for first, width in n_tiles(H):
+                acc = product(attn_codes, attn_scales, rt, wo_codes[:, g], wo_scales[:, g], first, width)
+                nc.vector.tensor_tensor(
+                    out=x_mid[:, rt, first : first + width],
+                    in0=acc[:, :width],
+                    in1=x_sb[:, rt, first : first + width],
+                    op=ALU.add,
+                )
+            nc.sync.dma_start(out=x_mid_out[rt * P : (rt + 1) * P, :], in_=x_mid[:, rt, :])
+
+        def square(rt):
+            squares = work.tile([P, H], BF16, name="squares")
+            nc.scalar.activation(out=squares[:], in_=x_mid[:, rt, :], func=ACT.Square, accum_out=sum_sq[:, rt : rt + 1])
+
+        def normalise_and_turn(rt):
+            h = work.tile([P, H], BF16, name="h")
+            nc.vector.scalar_tensor_tensor(
+                out=h[:],
+                in0=x_mid[:, rt, :],
+                scalar=rstd[:, rt : rt + 1],
+                in1=gains[:, model_of(rt), :],
+                op0=ALU.mult,
+                op1=ALU.mult,
+            )
+            turned = turned_pool.tile([P, PASSES * PACK, P], BF16, name="turned")
+            for plane in range(PASSES * PACK):
+                nc.tensor.transpose(turned[:, plane, :], h[:, plane * P : (plane + 1) * P], ident_bf16[:])
+            return turned
+
+        def group_h(turned):
+            grouped = rows_pool.tile([P, PASSES * P * PACK], BF16, name="rows_grouped", align_bytes=64)
+            nc.scalar.copy(
+                out=grouped[:].rearrange("p (c r t) -> p c r t", c=PASSES, t=PACK),
+                in_=turned[:].rearrange("p (c t) r -> p c r t", t=PACK),
+            )
+            return grouped
+
+        def gate_part(g, q, rt):
+            codes, scales = codes_of[(g, q, 0)]
+            result = result_pool.tile([P, UNIT], F32, name="result")
+            for first, width in n_tiles(UNIT):
+                acc = product(h_codes, h_scales, rt, codes, scales, first, width)
+                nc.scalar.activation(out=result[:, first : first + width], in_=acc[:, :width], func=ACT.Silu)
+            return result
+
+        def up_part(g, q, rt, result):
+            codes, scales = codes_of[(g, q, 1)]
+            for first, width in n_tiles(UNIT):
+                acc = product(h_codes, h_scales, rt, codes, scales, first, width)
+                nc.vector.tensor_tensor(
+                    out=result[:, first : first + width],
+                    in0=acc[:, :width],
+                    in1=result[:, first : first + width],
+                    op=ALU.mult,
+                )
+            nc.sync.dma_start(out=h_mlp_out[rt * P : (rt + 1) * P, q * UNIT : (q + 1) * UNIT], in_=result[:])
+
+        load(0)
+        nc.sync.dma_start(out=attn_sb[:], in_=attn.rearrange("(rt p) k -> p rt k", p=P))
+        for i in range(1, RAW_BUFS):
+            load(i)
+        nc.sync.dma_start(out=x_sb[:], in_=x.rearrange("(rt p) k -> p rt k", p=P))
+        for g in range(MODELS):
+            nc.sync.dma_start(out=gains[:, g, :], in_=ln2[g, :].partition_broadcast(P))
+
+        advance()
+        attn_grouped = [turn_attn(rt) for rt in range(ROW_TILES)]
+        advance()
+        for rt in range(ROW_TILES):
+            quantise_rows(attn_grouped[rt], attn_codes, attn_scales, rt)
+        advance_until_quantised(("o", 0, 0, 0, PASSES - 1))
+        first_product(0)
+        first_product(1)
+        advance()
+        first_product(2)
+        square(0)
+        square(1)
+        advance_until_quantised(("o", 1, 0, 0, PASSES - 1))
+        first_product(3)
+        square(2)
+        square(3)
+        advance()
+        nc.vector.tensor_scalar(out=variance[:], in0=sum_sq[:], scalar1=1.0 / H, scalar2=EPS, op0=ALU.mult, op1=ALU.add)
+        nc.scalar.sqrt(out=std[:], in_=variance[:])
+        advance()
+        nc.vector.reciprocal(out=rstd[:], in_=std[:])
+        h_turned = [normalise_and_turn(rt) for rt in (0, 1)]
+        advance()
+        h_grouped = [group_h(turned) for turned in h_turned]
+        h_turned = [normalise_and_turn(rt) for rt in (2, 3)]
+        advance()
+        h_grouped.extend([group_h(turned) for turned in h_turned])
+        quantise_rows(h_grouped[0], h_codes, h_scales, 0)
+        quantise_rows(h_grouped[1], h_codes, h_scales, 1)
+        advance()
+        quantise_rows(h_grouped[2], h_codes, h_scales, 2)
+        quantise_rows(h_grouped[3], h_codes, h_scales, 3)
+
+        jobs = [(g, q, rt) for g, q in groups for rt in range(ROW_TILES) if model_of(rt) == g]
+        open_job = None
+        for g, q, rt in jobs:
+            advance()
+            if open_job is not None:
+                up_part(*open_job)
+            advance_until_quantised(("gu", g, q, 0, PASSES - 1))
+            open_job = (g, q, rt, gate_part(g, q, rt))
+        advance_until_quantised(units[-1])
+        up_part(*open_job)

@@ -48,6 +48,7 @@ def tile_twomodelblockrouted_pb_kernel(tc, attn, x, W_o, W_gu, ln2, x_mid_out, h
         result_pool = stack.enter_context(tc.tile_pool(name="result", bufs=3))
         turned_pool = stack.enter_context(tc.psum_pool(name="turned", bufs=2))
         acc_pool = stack.enter_context(tc.psum_pool(name="acc", bufs=6))
+        stack.enter_context(tc.manual_schedule())
 
         ident_f32 = keep.tile([P, P], F32)
         make_identity(nc, ident_f32[:])

@@ -48,7 +48,6 @@ def tile_twomodelblockrouted_pb_kernel(tc, attn, x, W_o, W_gu, ln2, x_mid_out, h
         result_pool = stack.enter_context(tc.tile_pool(name="result", bufs=3))
         turned_pool = stack.enter_context(tc.psum_pool(name="turned", bufs=2))
         acc_pool = stack.enter_context(tc.psum_pool(name="acc", bufs=6))
-        stack.enter_context(tc.manual_schedule())
 
         ident_f32 = keep.tile([P, P], F32)
         make_identity(nc, ident_f32[:])
@@ -61,7 +60,7 @@ def tile_twomodelblockrouted_pb_kernel(tc, attn, x, W_o, W_gu, ln2, x_mid_out, h
 
         attn_sb = keep.tile([P, ROW_TILES, H], BF16)
         x_sb = keep.tile([P, ROW_TILES, H], BF16)
-        gains = keep.tile([P, MODELS, H], BF16)
+        gains = keep.tile([P, MODELS * H], BF16)
         x_mid = keep.tile([P, ROW_TILES, H], F32)
         attn_codes = keep.tile([P, ROW_TILES, PASSES * P], U32, align_bytes=64)
         attn_scales = keep.tile([P, ROW_TILES, PASSES * P], U8, align_bytes=64)
@@ -77,7 +76,7 @@ def tile_twomodelblockrouted_pb_kernel(tc, attn, x, W_o, W_gu, ln2, x_mid_out, h
         units = [("o", g, 0, 0, c) for g in range(MODELS) for c in range(PASSES)]
         groups = [(g, q) for g in range(MODELS) for q in range(FF // UNIT)]
         units.extend([("gu", g, q, half, c) for g, q in groups for half in range(2) for c in range(PASSES)])
-        stream = {"steps": 0}
+        stream = {"regrouped": 0, "quantised": 0}
         raw_of, grouped_of, codes_of = {}, {}, {}
 
         def width_of(i):
@@ -125,18 +124,23 @@ def tile_twomodelblockrouted_pb_kernel(tc, attn, x, W_o, W_gu, ln2, x_mid_out, h
                     in_=grouped_of[i][:, first:last, :].rearrange("p n t -> p (n t)"),
                 )
 
+        def flush():
+            while stream["quantised"] < stream["regrouped"]:
+                quantise(stream["quantised"])
+                stream["quantised"] += 1
+
         def advance():
-            step = stream["steps"]
-            stream["steps"] = step + 1
-            if step < len(units):
-                regroup(step)
-            if 1 <= step <= len(units):
-                quantise(step - 1)
-            if step + RAW_BUFS < len(units):
-                load(step + RAW_BUFS)
+            i = stream["regrouped"]
+            if i < len(units):
+                regroup(i)
+            flush()
+            if i < len(units):
+                stream["regrouped"] = i + 1
+            if i + RAW_BUFS < len(units):
+                load(i + RAW_BUFS)
 
         def advance_until_quantised(unit):
-            while stream["steps"] < units.index(unit) + 2:
+            while stream["quantised"] <= units.index(unit):
                 advance()
 
         def quantise_rows(grouped, codes, scales, rt):
@@ -190,7 +194,7 @@ def tile_twomodelblockrouted_pb_kernel(tc, attn, x, W_o, W_gu, ln2, x_mid_out, h
                 out=h[:],
                 in0=x_mid[:, rt, :],
                 scalar=rstd[:, rt : rt + 1],
-                in1=gains[:, model_of(rt), :],
+                in1=gains[:, model_of(rt) * H : (model_of(rt) + 1) * H],
                 op0=ALU.mult,
                 op1=ALU.mult,
             )
@@ -227,29 +231,39 @@ def tile_twomodelblockrouted_pb_kernel(tc, attn, x, W_o, W_gu, ln2, x_mid_out, h
                 )
             nc.sync.dma_start(out=h_mlp_out[rt * P : (rt + 1) * P, q * UNIT : (q + 1) * UNIT], in_=result[:])
 
+        gain_row = keep.tile([P, MODELS * H], BF16)
+        nc.vector.memset(gain_row[:].bitcast(mybir.dt.int32), 0)
+        ones = keep.tile([P, P], BF16)
+        nc.vector.memset(ones[:], 1.0)
+        nc.sync.dma_start(out=gain_row[0:1, :], in_=ln2.rearrange("(o g) k -> o (g k)", o=1))
         load(0)
+        load(1)
         nc.sync.dma_start(out=attn_sb[:], in_=attn.rearrange("(rt p) k -> p rt k", p=P))
-        for i in range(1, RAW_BUFS):
-            load(i)
         nc.sync.dma_start(out=x_sb[:], in_=x.rearrange("(rt p) k -> p rt k", p=P))
-        for g in range(MODELS):
-            nc.sync.dma_start(out=gains[:, g, :], in_=ln2[g, :].partition_broadcast(P))
+        load(2)
+        load(3)
+        for first, width in n_tiles(MODELS * H):
+            acc = acc_pool.tile([P, N_TILE], F32, name="acc")
+            nc.tensor.matmul(out=acc[:, :width], lhsT=ones[:], rhs=gain_row[:, first : first + width], start=True, stop=True)
+            nc.scalar.copy(out=gains[:, first : first + width], in_=acc[:, :width])
 
         advance()
-        attn_grouped = [turn_attn(rt) for rt in range(ROW_TILES)]
         advance()
+        attn_grouped = [turn_attn(rt) for rt in range(ROW_TILES)]
+        flush()
         for rt in range(ROW_TILES):
             quantise_rows(attn_grouped[rt], attn_codes, attn_scales, rt)
-        advance_until_quantised(("o", 0, 0, 0, PASSES - 1))
         first_product(0)
         first_product(1)
         advance()
         first_product(2)
         square(0)
         square(1)
-        advance_until_quantised(("o", 1, 0, 0, PASSES - 1))
-        first_product(3)
+        advance()
         square(2)
+        advance()
+        first_product(3)
+        advance()
         square(3)
         advance()
         nc.vector.tensor_scalar(out=variance[:], in0=sum_sq[:], scalar1=1.0 / H, scalar2=EPS, op0=ALU.mult, op1=ALU.add)
@@ -271,10 +285,10 @@ def tile_twomodelblockrouted_pb_kernel(tc, attn, x, W_o, W_gu, ln2, x_mid_out, h
         jobs = [(g, q, rt) for g, q in groups for rt in range(ROW_TILES) if model_of(rt) == g]
         open_job = None
         for g, q, rt in jobs:
+            advance_until_quantised(("gu", g, q, 0, PASSES - 1))
             advance()
             if open_job is not None:
                 up_part(*open_job)
-            advance_until_quantised(("gu", g, q, 0, PASSES - 1))
             open_job = (g, q, rt, gate_part(g, q, rt))
         advance_until_quantised(units[-1])
         up_part(*open_job)

@@ -22,7 +22,7 @@ ROW_TILES = ROWS // P
 N_TILE = 512
 QUANT_COLS = 1024
 UNIT = FF // 2
-RUN = 4
+RUN = 8
 RAW_BUFS = 4
 
 FLOPS = 2 * ROWS * H * H + 2 * ROWS * H * 2 * FF

@@ -51,8 +51,6 @@ def tile_twomodelblockrouted_pb_kernel(tc, attn, x, W_o, W_gu, ln2, x_mid_out, h
 
         ident_f32 = keep.tile([P, P], F32)
         make_identity(nc, ident_f32[:])
-        ident_bf16 = keep.tile([P, P], BF16)
-        make_identity(nc, ident_bf16[:])
         one = keep.tile([P, 1], F32)
         nc.vector.memset(one[:], 1.0)
         warm = keep.tile([P, 1], F32)
@@ -87,13 +85,11 @@ def tile_twomodelblockrouted_pb_kernel(tc, attn, x, W_o, W_gu, ln2, x_mid_out, h
             raw = raw_pool.tile([P, PACK, UNIT], BF16, name="raw")
             k_rows = slice(c * K_PASS, (c + 1) * K_PASS)
             if kind == "o":
-                for u in range(2):
-                    rows = W_o[g, c * K_PASS + u * 2 * P : c * K_PASS + (u + 1) * 2 * P, :]
-                    nc.sync.dma_start(out=raw[:, 2 * u : 2 * u + 2, :H], in_=rows.rearrange("(p e) n -> p e n", e=2))
+                rows = W_o[g, k_rows, :]
             else:
                 first = half * FF + q * UNIT
                 rows = W_gu[g, k_rows, first : first + UNIT]
-                nc.sync.dma_start(out=raw[:], in_=rows.rearrange("(t p) n -> p t n", p=P))
+            nc.sync.dma_start(out=raw[:, :, : width_of(i)], in_=rows.rearrange("(p t) n -> p t n", t=PACK))
             raw_of[i] = raw
 
         def regroup(i):
@@ -160,11 +156,15 @@ def tile_twomodelblockrouted_pb_kernel(tc, attn, x, W_o, W_gu, ln2, x_mid_out, h
                 )
             return acc
 
-        def turn_attn(rt):
-            words = attn_sb[:, rt, :].bitcast(F32)
+        def turn(words):
             turned = turned_pool.tile([P, PASSES * 2, P], F32, name="turned")
-            for plane in range(PASSES * 2):
-                nc.tensor.transpose(turned[:, plane, :], words[:, plane * P : (plane + 1) * P], ident_f32[:])
+            for c in range(PASSES):
+                for u in range(2):
+                    pairs = words[:, 2 * P * c + u : 2 * P * (c + 1) : 2]
+                    nc.tensor.transpose(turned[:, 2 * c + u, :], pairs, ident_f32[:])
+            return turned
+
+        def group_rows(turned):
             grouped = rows_pool.tile([P, PASSES * P * PACK], BF16, name="rows_grouped", align_bytes=64)
             nc.scalar.copy(
                 out=grouped[:].bitcast(F32).rearrange("p (c r u) -> p c r u", c=PASSES, u=2),
@@ -188,7 +188,7 @@ def tile_twomodelblockrouted_pb_kernel(tc, attn, x, W_o, W_gu, ln2, x_mid_out, h
             squares = work.tile([P, H], BF16, name="squares")
             nc.scalar.activation(out=squares[:], in_=x_mid[:, rt, :], func=ACT.Square, accum_out=sum_sq[:, rt : rt + 1])
 
-        def normalise_and_turn(rt):
+        def normalise(rt):
             h = work.tile([P, H], BF16, name="h")
             nc.vector.scalar_tensor_tensor(
                 out=h[:],
@@ -198,18 +198,7 @@ def tile_twomodelblockrouted_pb_kernel(tc, attn, x, W_o, W_gu, ln2, x_mid_out, h
                 op0=ALU.mult,
                 op1=ALU.mult,
             )
-            turned = turned_pool.tile([P, PASSES * PACK, P], BF16, name="turned")
-            for plane in range(PASSES * PACK):
-                nc.tensor.transpose(turned[:, plane, :], h[:, plane * P : (plane + 1) * P], ident_bf16[:])
-            return turned
-
-        def group_h(turned):
-            grouped = rows_pool.tile([P, PASSES * P * PACK], BF16, name="rows_grouped", align_bytes=64)
-            nc.scalar.copy(
-                out=grouped[:].rearrange("p (c r t) -> p c r t", c=PASSES, t=PACK),
-                in_=turned[:].rearrange("p (c t) r -> p c r t", t=PACK),
-            )
-            return grouped
+            return h
 
         def gate_part(g, q, rt):
             codes, scales = codes_of[(g, q, 0)]
@@ -249,7 +238,7 @@ def tile_twomodelblockrouted_pb_kernel(tc, attn, x, W_o, W_gu, ln2, x_mid_out, h
 
         advance()
         advance()
-        attn_grouped = [turn_attn(rt) for rt in range(ROW_TILES)]
+        attn_grouped = [group_rows(turn(attn_sb[:, rt, :].bitcast(F32))) for rt in range(ROW_TILES)]
         flush()
         for rt in range(ROW_TILES):
             quantise_rows(attn_grouped[rt], attn_codes, attn_scales, rt)
@@ -270,12 +259,12 @@ def tile_twomodelblockrouted_pb_kernel(tc, attn, x, W_o, W_gu, ln2, x_mid_out, h
         nc.scalar.sqrt(out=std[:], in_=variance[:])
         advance()
         nc.vector.reciprocal(out=rstd[:], in_=std[:])
-        h_turned = [normalise_and_turn(rt) for rt in (0, 1)]
+        h_turned = [turn(normalise(rt)[:].bitcast(F32)) for rt in (0, 1)]
         advance()
-        h_grouped = [group_h(turned) for turned in h_turned]
-        h_turned = [normalise_and_turn(rt) for rt in (2, 3)]
+        h_grouped = [group_rows(turned) for turned in h_turned]
+        h_turned = [turn(normalise(rt)[:].bitcast(F32)) for rt in (2, 3)]
         advance()
-        h_grouped.extend([group_h(turned) for turned in h_turned])
+        h_grouped.extend([group_rows(turned) for turned in h_turned])
         quantise_rows(h_grouped[0], h_codes, h_scales, 0)
         quantise_rows(h_grouped[1], h_codes, h_scales, 1)
         advance()

@@ -23,6 +23,7 @@ N_TILE = 512
 QUANT_COLS = 1024
 UNIT = FF // 2
 RUN = 8
+PE_COLS = 256
 RAW_BUFS = 4
 
 FLOPS = 2 * ROWS * H * H + 2 * ROWS * H * 2 * FF
@@ -46,11 +47,13 @@ def tile_twomodelblockrouted_pb_kernel(tc, attn, x, W_o, W_gu, ln2, x_mid_out, h
         work = stack.enter_context(tc.tile_pool(name="work", bufs=2))
         rows_pool = stack.enter_context(tc.tile_pool(name="rows", bufs=ROW_TILES))
         result_pool = stack.enter_context(tc.tile_pool(name="result", bufs=3))
-        turned_pool = stack.enter_context(tc.psum_pool(name="turned", bufs=2))
-        acc_pool = stack.enter_context(tc.psum_pool(name="acc", bufs=6))
+        turned_pool = stack.enter_context(tc.psum_pool(name="turned", bufs=3))
+        acc_pool = stack.enter_context(tc.psum_pool(name="acc", bufs=5))
 
         ident_f32 = keep.tile([P, P], F32)
         make_identity(nc, ident_f32[:])
+        ident_bf16 = keep.tile([P, P], BF16)
+        make_identity(nc, ident_bf16[:])
         one = keep.tile([P, 1], F32)
         nc.vector.memset(one[:], 1.0)
         warm = keep.tile([P, 1], F32)
@@ -94,8 +97,20 @@ def tile_twomodelblockrouted_pb_kernel(tc, attn, x, W_o, W_gu, ln2, x_mid_out, h
 
         def regroup(i):
             width = width_of(i)
+            direct = width - PE_COLS if units[i][0] == "gu" else width
             grouped = grouped_pool.tile([P, UNIT, PACK], BF16, name="grouped", align_bytes=64)
-            for copy, first, last in ((nc.vector.tensor_copy, 0, width // 2), (nc.scalar.copy, width // 2, width)):
+            if direct < width:
+                bank = turned_pool.tile([P, PE_COLS, PACK], BF16, name="turned")
+                for first in range(0, PE_COLS, P):
+                    nc.tensor.matmul(
+                        out=bank[:, first : first + P, :],
+                        lhsT=ident_bf16[:],
+                        rhs=raw_of[i][:, :, direct + first : direct + first + P].rearrange("p t n -> p n t"),
+                        start=True,
+                        stop=True,
+                    )
+                nc.scalar.copy(out=grouped[:, direct:width, :], in_=bank[:])
+            for copy, first, last in ((nc.vector.tensor_copy, 0, direct // 2), (nc.scalar.copy, direct // 2, direct)):
                 copy(
                     out=grouped[:, first:last, :].rearrange("p (c i) t -> p c t i", i=RUN),
                     in_=raw_of[i][:, :, first:last].rearrange("p t (c i) -> p c t i", i=RUN),

@@ -103,9 +103,9 @@ def tile_twomodelblockrouted_pb_kernel(tc, attn, x, W_o, W_gu, ln2, x_mid_out, h
                 bank = turned_pool.tile([P, PE_COLS, PACK], BF16, name="turned")
                 for first in range(0, PE_COLS, P):
                     nc.tensor.matmul(
-                        out=bank[:, first : first + P, :],
+                        out=bank[:, first : first + P, :].rearrange("p n t -> p t n"),
                         lhsT=ident_bf16[:],
-                        rhs=raw_of[i][:, :, direct + first : direct + first + P].rearrange("p t n -> p n t"),
+                        rhs=raw_of[i][:, :, direct + first : direct + first + P],
                         start=True,
                         stop=True,
                     )

@@ -5,6 +5,7 @@ from concourse.masks import make_identity
 
 F32 = mybir.dt.float32
 BF16 = mybir.dt.bfloat16
+I32 = mybir.dt.int32
 U32 = mybir.dt.uint32
 U8 = mybir.dt.uint8
 FP8X4 = mybir.dt.float8_e4m3fn_x4
@@ -20,11 +21,13 @@ MODELS = 2
 PASSES = H // K_PASS
 ROW_TILES = ROWS // P
 N_TILE = 512
-QUANT_COLS = 1024
 UNIT = FF // 2
+QUANT_COLS = 1024
 RUN = 8
 PE_COLS = 256
-RAW_BUFS = 4
+O_VECTOR_COLS, VECTOR_COLS = 512, 576
+RAW_BUFS = 5
+TILES_A_STEP = 3
 
 FLOPS = 2 * ROWS * H * H + 2 * ROWS * H * 2 * FF
 
@@ -33,8 +36,8 @@ def model_of(row_tile):
     return 0 if row_tile * P < SPLIT_ROW else 1
 
 
-def n_tiles(width):
-    return [(first, min(N_TILE, width - first)) for first in range(0, width, N_TILE)]
+def cut(width, piece):
+    return [(first, min(piece, width - first)) for first in range(0, width, piece)]
 
 
 def tile_twomodelblockrouted_pb_kernel(tc, attn, x, W_o, W_gu, ln2, x_mid_out, h_mlp_out):
@@ -43,13 +46,17 @@ def tile_twomodelblockrouted_pb_kernel(tc, attn, x, W_o, W_gu, ln2, x_mid_out, h
         keep = stack.enter_context(tc.tile_pool(name="keep", bufs=1))
         raw_pool = stack.enter_context(tc.tile_pool(name="raw", bufs=RAW_BUFS))
         grouped_pool = stack.enter_context(tc.tile_pool(name="grouped", bufs=3))
-        codes_pool = stack.enter_context(tc.tile_pool(name="codes", bufs=2))
+        gate_pool = stack.enter_context(tc.tile_pool(name="gate_codes", bufs=3))
+        up_pool = stack.enter_context(tc.tile_pool(name="up_codes", bufs=2))
         work = stack.enter_context(tc.tile_pool(name="work", bufs=2))
         rows_pool = stack.enter_context(tc.tile_pool(name="rows", bufs=ROW_TILES))
-        result_pool = stack.enter_context(tc.tile_pool(name="result", bufs=3))
-        turned_pool = stack.enter_context(tc.psum_pool(name="turned", bufs=3))
-        acc_pool = stack.enter_context(tc.psum_pool(name="acc", bufs=5))
+        result_pool = stack.enter_context(tc.tile_pool(name="result", bufs=ROW_TILES))
+        bank_pool = stack.enter_context(tc.psum_pool(name="bank", bufs=2))
+        acc_pool = stack.enter_context(tc.psum_pool(name="acc", bufs=6))
+        stack.enter_context(tc.manual_schedule())
 
+        gain_row = result_pool.tile([P, MODELS * H], BF16, name="result")
+        nc.gpsimd.memset(gain_row[:].bitcast(I32), 0)
         ident_f32 = keep.tile([P, P], F32)
         make_identity(nc, ident_f32[:])
         ident_bf16 = keep.tile([P, P], BF16)
@@ -58,101 +65,101 @@ def tile_twomodelblockrouted_pb_kernel(tc, attn, x, W_o, W_gu, ln2, x_mid_out, h
         nc.vector.memset(one[:], 1.0)
         warm = keep.tile([P, 1], F32)
         nc.scalar.sqrt(out=warm[:], in_=one[:])
+        ones = keep.tile([P, P], BF16)
+        nc.vector.memset(ones[:], 1.0)
 
-        attn_sb = keep.tile([P, ROW_TILES, H], BF16)
-        x_sb = keep.tile([P, ROW_TILES, H], BF16)
         gains = keep.tile([P, MODELS * H], BF16)
         x_mid = keep.tile([P, ROW_TILES, H], F32)
         attn_codes = keep.tile([P, ROW_TILES, PASSES * P], U32, align_bytes=64)
         attn_scales = keep.tile([P, ROW_TILES, PASSES * P], U8, align_bytes=64)
         h_codes = keep.tile([P, ROW_TILES, PASSES * P], U32, align_bytes=64)
         h_scales = keep.tile([P, ROW_TILES, PASSES * P], U8, align_bytes=64)
-        wo_codes = keep.tile([P, MODELS, PASSES, H], U32, align_bytes=64)
-        wo_scales = keep.tile([P, MODELS, PASSES, H], U8, align_bytes=64)
         sum_sq = keep.tile([P, ROW_TILES], F32)
         variance = keep.tile([P, ROW_TILES], F32)
         std = keep.tile([P, ROW_TILES], F32)
         rstd = keep.tile([P, ROW_TILES], F32)
 
-        units = [("o", g, 0, 0, c) for g in range(MODELS) for c in range(PASSES)]
-        groups = [(g, q) for g in range(MODELS) for q in range(FF // UNIT)]
-        units.extend([("gu", g, q, half, c) for g, q in groups for half in range(2) for c in range(PASSES)])
-        stream = {"regrouped": 0, "quantised": 0}
-        raw_of, grouped_of, codes_of = {}, {}, {}
+        wo_codes = keep.tile([P, MODELS, PASSES, H], U32, align_bytes=64)
+        wo_scales = keep.tile([P, MODELS, PASSES, H], U8, align_bytes=64)
+        attn_sb = gate_pool.tile([P, ROW_TILES, H], BF16, name="codes", align_bytes=64)
+        x_sb = up_pool.tile([P, ROW_TILES, H], BF16, name="codes", align_bytes=64)
 
-        def width_of(i):
-            return H if units[i][0] == "o" else UNIT
+        units = [("o", g, 0, H, 0, c) for g in range(MODELS) for c in range(PASSES)]
+        groups = [(g, start) for g in range(MODELS) for start in range(0, FF, UNIT)]
+        units.extend([("gu", g, start, UNIT, half, c) for g, start in groups for half in range(2) for c in range(PASSES)])
+        raw_of, bank_of, grouped_of, codes_of = {}, {}, {}, {}
 
         def load(i):
-            kind, g, q, half, c = units[i]
-            raw = raw_pool.tile([P, PACK, UNIT], BF16, name="raw")
+            if i >= len(units):
+                return
+            kind, g, start, width, half, c = units[i]
+            buffer = raw_pool.tile([P, PACK * UNIT], BF16, name="raw")
+            raw_of[i] = buffer[:, : PACK * width].rearrange("p (t n) -> p t n", t=PACK)
             k_rows = slice(c * K_PASS, (c + 1) * K_PASS)
             if kind == "o":
                 rows = W_o[g, k_rows, :]
             else:
-                first = half * FF + q * UNIT
-                rows = W_gu[g, k_rows, first : first + UNIT]
-            nc.sync.dma_start(out=raw[:, :, : width_of(i)], in_=rows.rearrange("(p t) n -> p t n", t=PACK))
-            raw_of[i] = raw
+                rows = W_gu[g, k_rows, half * FF + start : half * FF + start + width]
+            for first, cols in cut(width, width // 2 if i == 0 else width):
+                piece = rows[:, first : first + cols].rearrange("(p t) n -> p t n", t=PACK)
+                nc.sync.dma_start(out=raw_of[i][:, :, first : first + cols], in_=piece)
 
-        def regroup(i):
-            width = width_of(i)
-            direct = width - PE_COLS if units[i][0] == "gu" else width
+        def tensor_cols(i):
+            return PE_COLS if i < len(units) and units[i][0] == "gu" else 0
+
+        def tensor_regroup(i):
+            if tensor_cols(i) == 0:
+                return
+            direct = units[i][3] - PE_COLS
+            bank_of[i] = bank_pool.tile([P, PE_COLS, PACK], BF16, name="bank")
+            for first in range(0, PE_COLS, P):
+                nc.tensor.matmul(
+                    out=bank_of[i][:, first : first + P, :].rearrange("p n t -> p t n"),
+                    lhsT=ident_bf16[:],
+                    rhs=raw_of[i][:, :, direct + first : direct + first + P],
+                    start=True,
+                    stop=True,
+                )
+
+        def step(i):
+            if i >= len(units):
+                return
+            width = units[i][3]
+            direct = width - tensor_cols(i)
+            vector = O_VECTOR_COLS if units[i][0] == "o" else VECTOR_COLS
             grouped = grouped_pool.tile([P, UNIT, PACK], BF16, name="grouped", align_bytes=64)
             if direct < width:
-                bank = turned_pool.tile([P, PE_COLS, PACK], BF16, name="turned")
-                for first in range(0, PE_COLS, P):
-                    nc.tensor.matmul(
-                        out=bank[:, first : first + P, :].rearrange("p n t -> p t n"),
-                        lhsT=ident_bf16[:],
-                        rhs=raw_of[i][:, :, direct + first : direct + first + P],
-                        start=True,
-                        stop=True,
+                nc.scalar.copy(out=grouped[:, direct:width, :], in_=bank_of[i][:])
+            parts = 2 if i == 0 else 1
+            for start in range(0, direct, direct // parts):
+                middle, end = start + vector // parts, start + direct // parts
+                for copy, first, last in ((nc.vector.tensor_copy, start, middle), (nc.scalar.copy, middle, end)):
+                    copy(
+                        out=grouped[:, first:last, :].rearrange("p (c i) t -> p c t i", i=RUN),
+                        in_=raw_of[i][:, :, first:last].rearrange("p t (c i) -> p c t i", i=RUN),
                     )
-                nc.scalar.copy(out=grouped[:, direct:width, :], in_=bank[:])
-            for copy, first, last in ((nc.vector.tensor_copy, 0, direct // 2), (nc.scalar.copy, direct // 2, direct)):
-                copy(
-                    out=grouped[:, first:last, :].rearrange("p (c i) t -> p c t i", i=RUN),
-                    in_=raw_of[i][:, :, first:last].rearrange("p t (c i) -> p c t i", i=RUN),
-                )
             grouped_of[i] = grouped
+            load(i + RAW_BUFS)
 
         def quantise(i):
-            kind, g, q, half, c = units[i]
+            if i >= len(units):
+                return
+            kind, g, start, width, half, c = units[i]
             if kind == "o":
                 codes, scales = wo_codes[:, g, c, :], wo_scales[:, g, c, :]
             else:
                 if c == 0:
-                    half_codes = codes_pool.tile([P, PASSES, UNIT], U32, name="codes%d" % half, align_bytes=64)
-                    half_scales = codes_pool.tile([P, PASSES, UNIT], U8, name="scales%d" % half, align_bytes=64)
-                    codes_of[(g, q, half)] = (half_codes, half_scales)
-                codes, scales = codes_of[(g, q, half)][0][:, c, :], codes_of[(g, q, half)][1][:, c, :]
-            for first in range(0, width_of(i), QUANT_COLS):
-                last = min(first + QUANT_COLS, width_of(i))
+                    pool = (gate_pool, up_pool)[half]
+                    half_codes = pool.tile([P, PASSES, UNIT], U32, name="codes", align_bytes=64)
+                    half_scales = pool.tile([P, PASSES, UNIT], U8, name="scales", align_bytes=64)
+                    codes_of[(g, start, half)] = (half_codes, half_scales)
+                codes, scales = [plane[:, c, :] for plane in codes_of[(g, start, half)]]
+            for first, cols in cut(width, QUANT_COLS):
                 nc.vector.quantize_mx(
-                    out=codes[:, first:last].bitcast(FP8X4),
-                    scales=scales[:, first:last],
-                    in_=grouped_of[i][:, first:last, :].rearrange("p n t -> p (n t)"),
+                    out=codes[:, first : first + cols].bitcast(FP8X4),
+                    scales=scales[:, first : first + cols],
+                    in_=grouped_of[i][:, first : first + cols, :].rearrange("p n t -> p (n t)"),
                 )
-
-        def flush():
-            while stream["quantised"] < stream["regrouped"]:
-                quantise(stream["quantised"])
-                stream["quantised"] += 1
-
-        def advance():
-            i = stream["regrouped"]
-            if i < len(units):
-                regroup(i)
-            flush()
-            if i < len(units):
-                stream["regrouped"] = i + 1
-            if i + RAW_BUFS < len(units):
-                load(i + RAW_BUFS)
-
-        def advance_until_quantised(unit):
-            while stream["quantised"] <= units.index(unit):
-                advance()
 
         def quantise_rows(grouped, codes, scales, rt):
             nc.vector.quantize_mx(out=codes[:, rt, :].bitcast(FP8X4), scales=scales[:, rt, :], in_=grouped[:])
@@ -172,7 +179,7 @@ def tile_twomodelblockrouted_pb_kernel(tc, attn, x, W_o, W_gu, ln2, x_mid_out, h
             return acc
 
         def turn(words):
-            turned = turned_pool.tile([P, PASSES * 2, P], F32, name="turned")
+            turned = bank_pool.tile([P, PASSES * 2, P], F32, name="bank")
             for c in range(PASSES):
                 for u in range(2):
                     pairs = words[:, 2 * P * c + u : 2 * P * (c + 1) : 2]
@@ -189,15 +196,15 @@ def tile_twomodelblockrouted_pb_kernel(tc, attn, x, W_o, W_gu, ln2, x_mid_out, h
 
         def first_product(rt):
             g = model_of(rt)
-            for first, width in n_tiles(H):
-                acc = product(attn_codes, attn_scales, rt, wo_codes[:, g], wo_scales[:, g], first, width)
-                nc.vector.tensor_tensor(
-                    out=x_mid[:, rt, first : first + width],
-                    in0=acc[:, :width],
-                    in1=x_sb[:, rt, first : first + width],
-                    op=ALU.add,
-                )
-            nc.sync.dma_start(out=x_mid_out[rt * P : (rt + 1) * P, :], in_=x_mid[:, rt, :])
+            return [
+                product(attn_codes, attn_scales, rt, wo_codes[:, g], wo_scales[:, g], first, N_TILE)
+                for first in range(0, H, N_TILE)
+            ]
+
+        def add_x(rt, accs):
+            for n, acc in enumerate(accs):
+                cols = slice(n * N_TILE, (n + 1) * N_TILE)
+                nc.vector.tensor_tensor(out=x_mid[:, rt, cols], in0=acc[:], in1=x_sb[:, rt, cols], op=ALU.add)
 
         def square(rt):
             squares = work.tile([P, H], BF16, name="squares")
@@ -215,84 +222,119 @@ def tile_twomodelblockrouted_pb_kernel(tc, attn, x, W_o, W_gu, ln2, x_mid_out, h
             )
             return h
 
-        def gate_part(g, q, rt):
-            codes, scales = codes_of[(g, q, 0)]
-            result = result_pool.tile([P, UNIT], F32, name="result")
-            for first, width in n_tiles(UNIT):
-                acc = product(h_codes, h_scales, rt, codes, scales, first, width)
-                nc.scalar.activation(out=result[:, first : first + width], in_=acc[:, :width], func=ACT.Silu)
-            return result
-
-        def up_part(g, q, rt, result):
-            codes, scales = codes_of[(g, q, 1)]
-            for first, width in n_tiles(UNIT):
-                acc = product(h_codes, h_scales, rt, codes, scales, first, width)
-                nc.vector.tensor_tensor(
-                    out=result[:, first : first + width],
-                    in0=acc[:, :width],
-                    in1=result[:, first : first + width],
-                    op=ALU.mult,
-                )
-            nc.sync.dma_start(out=h_mlp_out[rt * P : (rt + 1) * P, q * UNIT : (q + 1) * UNIT], in_=result[:])
-
-        gain_row = keep.tile([P, MODELS * H], BF16)
-        nc.vector.memset(gain_row[:].bitcast(mybir.dt.int32), 0)
-        ones = keep.tile([P, P], BF16)
-        nc.vector.memset(ones[:], 1.0)
-        nc.sync.dma_start(out=gain_row[0:1, :], in_=ln2.rearrange("(o g) k -> o (g k)", o=1))
         load(0)
+        nc.sync.dma_start(out=gain_row[0:1, :], in_=ln2.rearrange("(o g) k -> o (g k)", o=1))
         load(1)
-        nc.sync.dma_start(out=attn_sb[:], in_=attn.rearrange("(rt p) k -> p rt k", p=P))
-        nc.sync.dma_start(out=x_sb[:], in_=x.rearrange("(rt p) k -> p rt k", p=P))
         load(2)
+        nc.sync.dma_start(out=attn_sb[:], in_=attn.rearrange("(rt p) k -> p rt k", p=P))
         load(3)
-        for first, width in n_tiles(MODELS * H):
-            acc = acc_pool.tile([P, N_TILE], F32, name="acc")
-            nc.tensor.matmul(out=acc[:, :width], lhsT=ones[:], rhs=gain_row[:, first : first + width], start=True, stop=True)
-            nc.scalar.copy(out=gains[:, first : first + width], in_=acc[:, :width])
+        nc.sync.dma_start(out=x_sb[:], in_=x.rearrange("(rt p) k -> p rt k", p=P))
+        load(4)
 
-        advance()
-        advance()
+        step(0)
+        quantise(0)
+        step(1)
+        for g in range(MODELS):
+            bank = bank_pool.tile([P, H], BF16, name="bank")
+            for first in range(0, H, N_TILE):
+                row = gain_row[:, g * H + first : g * H + first + N_TILE]
+                nc.tensor.matmul(out=bank[:, first : first + N_TILE], lhsT=ones[:], rhs=row, start=True, stop=True)
+            nc.scalar.copy(out=gains[:, g * H : (g + 1) * H], in_=bank[:])
+        quantise(1)
+        step(2)
         attn_grouped = [group_rows(turn(attn_sb[:, rt, :].bitcast(F32))) for rt in range(ROW_TILES)]
-        flush()
+        quantise(2)
         for rt in range(ROW_TILES):
             quantise_rows(attn_grouped[rt], attn_codes, attn_scales, rt)
-        first_product(0)
-        first_product(1)
-        advance()
-        first_product(2)
+        step(3)
+        accs = [first_product(rt) for rt in (0, 1, 2)]
+        add_x(0, accs[0])
         square(0)
+        quantise(3)
+        add_x(1, accs[1])
         square(1)
-        advance()
+        add_x(2, accs[2])
+        accs.append(first_product(3))
+        tensor_regroup(4)
+        step(4)
         square(2)
-        advance()
-        first_product(3)
-        advance()
+        add_x(3, accs[3])
+        tensor_regroup(5)
+        step(5)
         square(3)
-        advance()
+        quantise(4)
+        tensor_regroup(6)
+        step(6)
+        quantise(5)
         nc.vector.tensor_scalar(out=variance[:], in0=sum_sq[:], scalar1=1.0 / H, scalar2=EPS, op0=ALU.mult, op1=ALU.add)
         nc.scalar.sqrt(out=std[:], in_=variance[:])
-        advance()
+        tensor_regroup(7)
+        step(7)
+        quantise(6)
         nc.vector.reciprocal(out=rstd[:], in_=std[:])
-        h_turned = [turn(normalise(rt)[:].bitcast(F32)) for rt in (0, 1)]
-        advance()
+        h_rows = [normalise(rt) for rt in (0, 1)]
+        tensor_regroup(8)
+        step(8)
+        h_turned = [turn(h[:].bitcast(F32)) for h in h_rows]
+        quantise(7)
         h_grouped = [group_rows(turned) for turned in h_turned]
-        h_turned = [turn(normalise(rt)[:].bitcast(F32)) for rt in (2, 3)]
-        advance()
+        h_rows = [normalise(rt) for rt in (2, 3)]
+        tensor_regroup(9)
+        step(9)
+        h_turned = [turn(h[:].bitcast(F32)) for h in h_rows]
+        quantise(8)
         h_grouped.extend([group_rows(turned) for turned in h_turned])
         quantise_rows(h_grouped[0], h_codes, h_scales, 0)
         quantise_rows(h_grouped[1], h_codes, h_scales, 1)
-        advance()
+        tensor_regroup(10)
+        step(10)
+        quantise(9)
         quantise_rows(h_grouped[2], h_codes, h_scales, 2)
         quantise_rows(h_grouped[3], h_codes, h_scales, 3)
+        tensor_regroup(11)
 
-        jobs = [(g, q, rt) for g, q in groups for rt in range(ROW_TILES) if model_of(rt) == g]
-        open_job = None
-        for g, q, rt in jobs:
-            advance_until_quantised(("gu", g, q, 0, PASSES - 1))
-            advance()
-            if open_job is not None:
-                up_part(*open_job)
-            open_job = (g, q, rt, gate_part(g, q, rt))
-        advance_until_quantised(units[-1])
-        up_part(*open_job)
+        open_tiles = ([], [])
+        results = {}
+
+        def open_by(i):
+            kind, g, start, width, half, c = units[i]
+            if kind == "gu" and c == PASSES - 1:
+                row_tiles = [rt for rt in range(ROW_TILES) if model_of(rt) == g]
+                open_tiles[half].extend([(g, start, rt) + piece for rt in row_tiles for piece in cut(UNIT, N_TILE)])
+
+        def second_product(half, g, start, rt, first, cols):
+            codes, scales = codes_of[(g, start, half)]
+            return product(h_codes, h_scales, rt, codes, scales, first, cols)
+
+        for i in range(10):
+            open_by(i)
+        gates_done = ups_done = 0
+        i = 11
+        while i <= len(units) or ups_done < len(open_tiles[1]):
+            gates = open_tiles[0][gates_done : gates_done + TILES_A_STEP]
+            ups = open_tiles[1][ups_done : min(ups_done + TILES_A_STEP, gates_done)]
+            gate_accs = [second_product(0, *tile) for tile in gates]
+            up_accs = [second_product(1, *tile) for tile in ups]
+            tensor_regroup(i + 1)
+            step(i)
+            for (g, start, rt, first, cols), acc in zip(gates, gate_accs):
+                if first == 0:
+                    results[(start, rt)] = result_pool.tile([P, UNIT], F32, name="result")
+                nc.scalar.activation(
+                    out=results[(start, rt)][:, first : first + cols], in_=acc[:, :cols], func=ACT.Silu
+                )
+            quantise(i - 1)
+            if i - 1 < len(units):
+                open_by(i - 1)
+            for (g, start, rt, first, cols), acc in zip(ups, up_accs):
+                result = results[(start, rt)]
+                piece = result[:, first : first + cols]
+                nc.vector.tensor_tensor(out=piece, in0=acc[:, :cols], in1=piece, op=ALU.mult)
+                if first + cols == UNIT:
+                    nc.sync.dma_start(out=h_mlp_out[rt * P : (rt + 1) * P, start : start + UNIT], in_=result[:])
+            if i in (12, 13, 14, 15):
+                rt = i - 12
+                nc.sync.dma_start(out=x_mid_out[rt * P : (rt + 1) * P, :], in_=x_mid[:, rt, :])
+            gates_done += len(gates)
+            ups_done += len(ups)
+            i += 1

@@ -25,7 +25,7 @@ UNIT = FF // 2
 QUANT_COLS = 1024
 RUN = 8
 PE_COLS = 256
-O_VECTOR_COLS, VECTOR_COLS = 512, 576
+O_VECTOR_COLS, VECTOR_COLS = 512, 544
 RAW_BUFS = 5
 TILES_A_STEP = 3
 
@@ -61,14 +61,13 @@ def tile_twomodelblockrouted_pb_kernel(tc, attn, x, W_o, W_gu, ln2, x_mid_out, h
         make_identity(nc, ident_f32[:])
         ident_bf16 = keep.tile([P, P], BF16)
         make_identity(nc, ident_bf16[:])
-        one = keep.tile([P, 1], F32)
-        nc.vector.memset(one[:], 1.0)
+        minus_half = keep.tile([P, ROW_TILES], F32)
+        nc.vector.memset(minus_half[:], -0.5)
         warm = keep.tile([P, 1], F32)
-        nc.scalar.sqrt(out=warm[:], in_=one[:])
+        nc.scalar.activation(out=warm[:], in_=minus_half[:, 0:1], func=ACT.Silu)
         ones = keep.tile([P, P], BF16)
         nc.vector.memset(ones[:], 1.0)
 
-        gains = keep.tile([P, MODELS * H], BF16)
         x_mid = keep.tile([P, ROW_TILES, H], F32)
         attn_codes = keep.tile([P, ROW_TILES, PASSES * P], U32, align_bytes=64)
         attn_scales = keep.tile([P, ROW_TILES, PASSES * P], U8, align_bytes=64)
@@ -76,7 +75,6 @@ def tile_twomodelblockrouted_pb_kernel(tc, attn, x, W_o, W_gu, ln2, x_mid_out, h
         h_scales = keep.tile([P, ROW_TILES, PASSES * P], U8, align_bytes=64)
         sum_sq = keep.tile([P, ROW_TILES], F32)
         variance = keep.tile([P, ROW_TILES], F32)
-        std = keep.tile([P, ROW_TILES], F32)
         rstd = keep.tile([P, ROW_TILES], F32)
 
         wo_codes = keep.tile([P, MODELS, PASSES, H], U32, align_bytes=64)
@@ -100,9 +98,7 @@ def tile_twomodelblockrouted_pb_kernel(tc, attn, x, W_o, W_gu, ln2, x_mid_out, h
                 rows = W_o[g, k_rows, :]
             else:
                 rows = W_gu[g, k_rows, half * FF + start : half * FF + start + width]
-            for first, cols in cut(width, width // 2 if i == 0 else width):
-                piece = rows[:, first : first + cols].rearrange("(p t) n -> p t n", t=PACK)
-                nc.sync.dma_start(out=raw_of[i][:, :, first : first + cols], in_=piece)
+            nc.sync.dma_start(out=raw_of[i], in_=rows.rearrange("(p t) n -> p t n", t=PACK))
 
         def tensor_cols(i):
             return PE_COLS if i < len(units) and units[i][0] == "gu" else 0
@@ -130,14 +126,11 @@ def tile_twomodelblockrouted_pb_kernel(tc, attn, x, W_o, W_gu, ln2, x_mid_out, h
             grouped = grouped_pool.tile([P, UNIT, PACK], BF16, name="grouped", align_bytes=64)
             if direct < width:
                 nc.scalar.copy(out=grouped[:, direct:width, :], in_=bank_of[i][:])
-            parts = 2 if i == 0 else 1
-            for start in range(0, direct, direct // parts):
-                middle, end = start + vector // parts, start + direct // parts
-                for copy, first, last in ((nc.vector.tensor_copy, start, middle), (nc.scalar.copy, middle, end)):
-                    copy(
-                        out=grouped[:, first:last, :].rearrange("p (c i) t -> p c t i", i=RUN),
-                        in_=raw_of[i][:, :, first:last].rearrange("p t (c i) -> p c t i", i=RUN),
-                    )
+            for copy, first, last in ((nc.vector.tensor_copy, 0, vector), (nc.scalar.copy, vector, direct)):
+                copy(
+                    out=grouped[:, first:last, :].rearrange("p (c i) t -> p c t i", i=RUN),
+                    in_=raw_of[i][:, :, first:last].rearrange("p t (c i) -> p c t i", i=RUN),
+                )
             grouped_of[i] = grouped
             load(i + RAW_BUFS)
 
@@ -154,7 +147,7 @@ def tile_twomodelblockrouted_pb_kernel(tc, attn, x, W_o, W_gu, ln2, x_mid_out, h
                     half_scales = pool.tile([P, PASSES, UNIT], U8, name="scales", align_bytes=64)
                     codes_of[(g, start, half)] = (half_codes, half_scales)
                 codes, scales = [plane[:, c, :] for plane in codes_of[(g, start, half)]]
-            for first, cols in cut(width, QUANT_COLS):
+            for first, cols in cut(width, QUANT_COLS if i + 1 < len(units) else N_TILE):
                 nc.vector.quantize_mx(
                     out=codes[:, first : first + cols].bitcast(FP8X4),
                     scales=scales[:, first : first + cols],
@@ -210,13 +203,20 @@ def tile_twomodelblockrouted_pb_kernel(tc, attn, x, W_o, W_gu, ln2, x_mid_out, h
             squares = work.tile([P, H], BF16, name="squares")
             nc.scalar.activation(out=squares[:], in_=x_mid[:, rt, :], func=ACT.Square, accum_out=sum_sq[:, rt : rt + 1])
 
-        def normalise(rt):
+        def spread_gains(g):
+            gains = acc_pool.tile([P, H], BF16, name="acc")
+            for first in range(0, H, N_TILE):
+                row = gain_row[:, g * H + first : g * H + first + N_TILE]
+                nc.tensor.matmul(out=gains[:, first : first + N_TILE], lhsT=ones[:], rhs=row, start=True, stop=True)
+            return gains
+
+        def normalise(rt, gains):
             h = work.tile([P, H], BF16, name="h")
             nc.vector.scalar_tensor_tensor(
                 out=h[:],
                 in0=x_mid[:, rt, :],
                 scalar=rstd[:, rt : rt + 1],
-                in1=gains[:, model_of(rt) * H : (model_of(rt) + 1) * H],
+                in1=gains[:],
                 op0=ALU.mult,
                 op1=ALU.mult,
             )
@@ -234,12 +234,6 @@ def tile_twomodelblockrouted_pb_kernel(tc, attn, x, W_o, W_gu, ln2, x_mid_out, h
         step(0)
         quantise(0)
         step(1)
-        for g in range(MODELS):
-            bank = bank_pool.tile([P, H], BF16, name="bank")
-            for first in range(0, H, N_TILE):
-                row = gain_row[:, g * H + first : g * H + first + N_TILE]
-                nc.tensor.matmul(out=bank[:, first : first + N_TILE], lhsT=ones[:], rhs=row, start=True, stop=True)
-            nc.scalar.copy(out=gains[:, g * H : (g + 1) * H], in_=bank[:])
         quantise(1)
         step(2)
         attn_grouped = [group_rows(turn(attn_sb[:, rt, :].bitcast(F32))) for rt in range(ROW_TILES)]
@@ -266,19 +260,19 @@ def tile_twomodelblockrouted_pb_kernel(tc, attn, x, W_o, W_gu, ln2, x_mid_out, h
         tensor_regroup(6)
         step(6)
         quantise(5)
-        nc.vector.tensor_scalar(out=variance[:], in0=sum_sq[:], scalar1=1.0 / H, scalar2=EPS, op0=ALU.mult, op1=ALU.add)
-        nc.scalar.sqrt(out=std[:], in_=variance[:])
+        nc.gpsimd.tensor_scalar(out=variance[:], in0=sum_sq[:], scalar1=1.0 / H, scalar2=EPS, op0=ALU.mult, op1=ALU.add)
+        nc.gpsimd.tensor_tensor(out=rstd[:], in0=variance[:], in1=minus_half[:], op=ALU.pow)
         tensor_regroup(7)
         step(7)
         quantise(6)
-        nc.vector.reciprocal(out=rstd[:], in_=std[:])
-        h_rows = [normalise(rt) for rt in (0, 1)]
+        gains = [spread_gains(g) for g in range(MODELS)]
+        h_rows = [normalise(rt, gains[0]) for rt in (0, 1)]
         tensor_regroup(8)
         step(8)
         h_turned = [turn(h[:].bitcast(F32)) for h in h_rows]
         quantise(7)
         h_grouped = [group_rows(turned) for turned in h_turned]
-        h_rows = [normalise(rt) for rt in (2, 3)]
+        h_rows = [normalise(2, gains[0]), normalise(3, gains[1])]
         tensor_regroup(9)
         step(9)
         h_turned = [turn(h[:].bitcast(F32)) for h in h_rows]
@@ -330,7 +324,9 @@ def tile_twomodelblockrouted_pb_kernel(tc, attn, x, W_o, W_gu, ln2, x_mid_out, h
                 result = results[(start, rt)]
                 piece = result[:, first : first + cols]
                 nc.vector.tensor_tensor(out=piece, in0=acc[:, :cols], in1=piece, op=ALU.mult)
-                if first + cols == UNIT:
+                if (g, start) == groups[-1]:
+                    nc.sync.dma_start(out=h_mlp_out[rt * P : (rt + 1) * P, start + first : start + first + cols], in_=piece)
+                elif first + cols == UNIT:
                     nc.sync.dma_start(out=h_mlp_out[rt * P : (rt + 1) * P, start : start + UNIT], in_=result[:])
             if i in (12, 13, 14, 15):
                 rt = i - 12

@@ -27,13 +27,24 @@ RUN = 8
 PE_COLS = 256
 O_VECTOR_COLS, VECTOR_COLS = 512, 544
 RAW_BUFS = 5
+X_MID_STEP = 12
 TILES_A_STEP = 3
 
 FLOPS = 2 * ROWS * H * H + 2 * ROWS * H * 2 * FF
 
 
+ROW_TILES_0 = SPLIT_ROW // P
+
+
 def model_of(row_tile):
-    return 0 if row_tile * P < SPLIT_ROW else 1
+    return 0 if row_tile < ROW_TILES_0 else 1
+
+
+def by_row_tile(rows):
+    return (
+        rows[:SPLIT_ROW, :].rearrange("(p rt) n -> p rt n", rt=ROW_TILES_0),
+        rows[SPLIT_ROW:, :].rearrange("(p rt) n -> p rt n", rt=1),
+    )
 
 
 def cut(width, piece):
@@ -222,13 +233,22 @@ def tile_twomodelblockrouted_pb_kernel(tc, attn, x, W_o, W_gu, ln2, x_mid_out, h
             )
             return h
 
+        def load_rows(tile, rows):
+            first, last = by_row_tile(rows)
+            nc.sync.dma_start(out=tile[:, :ROW_TILES_0, :], in_=first)
+            nc.sync.dma_start(out=tile[:, ROW_TILES_0:, :], in_=last)
+
+        def rows_of(out, rt):
+            first, last = by_row_tile(out)
+            return first[:, rt, :] if rt < ROW_TILES_0 else last[:, 0, :]
+
         load(0)
         nc.sync.dma_start(out=gain_row[0:1, :], in_=ln2.rearrange("(o g) k -> o (g k)", o=1))
         load(1)
         load(2)
-        nc.sync.dma_start(out=attn_sb[:], in_=attn.rearrange("(rt p) k -> p rt k", p=P))
+        load_rows(attn_sb, attn)
         load(3)
-        nc.sync.dma_start(out=x_sb[:], in_=x.rearrange("(rt p) k -> p rt k", p=P))
+        load_rows(x_sb, x)
         load(4)
 
         step(0)
@@ -325,12 +345,13 @@ def tile_twomodelblockrouted_pb_kernel(tc, attn, x, W_o, W_gu, ln2, x_mid_out, h
                 piece = result[:, first : first + cols]
                 nc.vector.tensor_tensor(out=piece, in0=acc[:, :cols], in1=piece, op=ALU.mult)
                 if (g, start) == groups[-1]:
-                    nc.sync.dma_start(out=h_mlp_out[rt * P : (rt + 1) * P, start + first : start + first + cols], in_=piece)
+                    nc.sync.dma_start(out=rows_of(h_mlp_out, rt)[:, start + first : start + first + cols], in_=piece)
                 elif first + cols == UNIT:
-                    nc.sync.dma_start(out=h_mlp_out[rt * P : (rt + 1) * P, start : start + UNIT], in_=result[:])
-            if i in (12, 13, 14, 15):
-                rt = i - 12
-                nc.sync.dma_start(out=x_mid_out[rt * P : (rt + 1) * P, :], in_=x_mid[:, rt, :])
+                    nc.sync.dma_start(out=rows_of(h_mlp_out, rt)[:, start : start + UNIT], in_=result[:])
+            if i == X_MID_STEP:
+                first, last = by_row_tile(x_mid_out)
+                nc.sync.dma_start(out=first, in_=x_mid[:, :ROW_TILES_0, :])
+                nc.sync.dma_start(out=last, in_=x_mid[:, ROW_TILES_0:, :])
             gates_done += len(gates)
             ups_done += len(ups)
             i += 1

@@ -25,7 +25,8 @@ UNIT = FF // 2
 QUANT_COLS = 1024
 RUN = 8
 PE_COLS = 256
-O_VECTOR_COLS, VECTOR_COLS = 512, 544
+O_VECTOR_COLS, VECTOR_COLS = 512, 528
+FIRST_GROUP_VECTOR_COLS = 608
 RAW_BUFS = 5
 X_MID_STEP = 12
 TILES_A_STEP = 3
@@ -133,7 +134,8 @@ def tile_twomodelblockrouted_pb_kernel(tc, attn, x, W_o, W_gu, ln2, x_mid_out, h
                 return
             width = units[i][3]
             direct = width - tensor_cols(i)
-            vector = O_VECTOR_COLS if units[i][0] == "o" else VECTOR_COLS
+            kind, g, begin = units[i][:3]
+            vector = O_VECTOR_COLS if kind == "o" else FIRST_GROUP_VECTOR_COLS if (g, begin) == groups[0] else VECTOR_COLS
             grouped = grouped_pool.tile([P, UNIT, PACK], BF16, name="grouped", align_bytes=64)
             if direct < width:
                 nc.scalar.copy(out=grouped[:, direct:width, :], in_=bank_of[i][:])

@@ -25,10 +25,11 @@ UNIT = FF // 2
 QUANT_COLS = 1024
 RUN = 8
 PE_COLS = 256
-O_VECTOR_COLS, VECTOR_COLS = 512, 528
-FIRST_GROUP_VECTOR_COLS = 608
+O_VECTOR_COLS, VECTOR_COLS = 512, 512
+FIRST_GROUP_VECTOR_COLS = 576
 RAW_BUFS = 5
 X_MID_STEP = 12
+RESULT_BUFS = 5
 TILES_A_STEP = 3
 
 FLOPS = 2 * ROWS * H * H + 2 * ROWS * H * 2 * FF
@@ -62,7 +63,7 @@ def tile_twomodelblockrouted_pb_kernel(tc, attn, x, W_o, W_gu, ln2, x_mid_out, h
         up_pool = stack.enter_context(tc.tile_pool(name="up_codes", bufs=2))
         work = stack.enter_context(tc.tile_pool(name="work", bufs=2))
         rows_pool = stack.enter_context(tc.tile_pool(name="rows", bufs=ROW_TILES))
-        result_pool = stack.enter_context(tc.tile_pool(name="result", bufs=ROW_TILES))
+        result_pool = stack.enter_context(tc.tile_pool(name="result", bufs=RESULT_BUFS))
         bank_pool = stack.enter_context(tc.psum_pool(name="bank", bufs=2))
         acc_pool = stack.enter_context(tc.psum_pool(name="acc", bufs=6))
         stack.enter_context(tc.manual_schedule())
@@ -184,8 +185,8 @@ def tile_twomodelblockrouted_pb_kernel(tc, attn, x, W_o, W_gu, ln2, x_mid_out, h
                 )
             return acc
 
-        def turn(words):
-            turned = bank_pool.tile([P, PASSES * 2, P], F32, name="bank")
+        def turn(words, pool, tag):
+            turned = pool.tile([P, PASSES * 2, P], F32, name=tag)
             for c in range(PASSES):
                 for u in range(2):
                     pairs = words[:, 2 * P * c + u : 2 * P * (c + 1) : 2]
@@ -258,7 +259,7 @@ def tile_twomodelblockrouted_pb_kernel(tc, attn, x, W_o, W_gu, ln2, x_mid_out, h
         step(1)
         quantise(1)
         step(2)
-        attn_grouped = [group_rows(turn(attn_sb[:, rt, :].bitcast(F32))) for rt in range(ROW_TILES)]
+        attn_grouped = [group_rows(turn(attn_sb[:, rt, :].bitcast(F32), bank_pool, "bank")) for rt in range(ROW_TILES)]
         quantise(2)
         for rt in range(ROW_TILES):
             quantise_rows(attn_grouped[rt], attn_codes, attn_scales, rt)
@@ -275,39 +276,36 @@ def tile_twomodelblockrouted_pb_kernel(tc, attn, x, W_o, W_gu, ln2, x_mid_out, h
         step(4)
         square(2)
         add_x(3, accs[3])
+        square(3)
         tensor_regroup(5)
         step(5)
-        square(3)
         quantise(4)
+        nc.gpsimd.tensor_scalar(out=variance[:], in0=sum_sq[:], scalar1=1.0 / H, scalar2=EPS, op0=ALU.mult, op1=ALU.add)
+        nc.gpsimd.tensor_tensor(out=rstd[:], in0=variance[:], in1=minus_half[:], op=ALU.pow)
         tensor_regroup(6)
         step(6)
         quantise(5)
-        nc.gpsimd.tensor_scalar(out=variance[:], in0=sum_sq[:], scalar1=1.0 / H, scalar2=EPS, op0=ALU.mult, op1=ALU.add)
-        nc.gpsimd.tensor_tensor(out=rstd[:], in0=variance[:], in1=minus_half[:], op=ALU.pow)
-        tensor_regroup(7)
-        step(7)
-        quantise(6)
         gains = [spread_gains(g) for g in range(MODELS)]
         h_rows = [normalise(rt, gains[0]) for rt in (0, 1)]
-        tensor_regroup(8)
-        step(8)
-        h_turned = [turn(h[:].bitcast(F32)) for h in h_rows]
-        quantise(7)
+        tensor_regroup(7)
+        step(7)
+        h_turned = [turn(h[:].bitcast(F32), acc_pool, "acc") for h in h_rows]
+        quantise(6)
         h_grouped = [group_rows(turned) for turned in h_turned]
         h_rows = [normalise(2, gains[0]), normalise(3, gains[1])]
-        tensor_regroup(9)
-        step(9)
-        h_turned = [turn(h[:].bitcast(F32)) for h in h_rows]
-        quantise(8)
+        tensor_regroup(8)
+        step(8)
+        h_turned = [turn(h[:].bitcast(F32), acc_pool, "acc") for h in h_rows]
+        quantise(7)
         h_grouped.extend([group_rows(turned) for turned in h_turned])
         quantise_rows(h_grouped[0], h_codes, h_scales, 0)
         quantise_rows(h_grouped[1], h_codes, h_scales, 1)
-        tensor_regroup(10)
-        step(10)
-        quantise(9)
+        tensor_regroup(9)
+        step(9)
+        quantise(8)
         quantise_rows(h_grouped[2], h_codes, h_scales, 2)
         quantise_rows(h_grouped[3], h_codes, h_scales, 3)
-        tensor_regroup(11)
+        tensor_regroup(10)
 
         open_tiles = ([], [])
         results = {}
@@ -322,10 +320,10 @@ def tile_twomodelblockrouted_pb_kernel(tc, attn, x, W_o, W_gu, ln2, x_mid_out, h
             codes, scales = codes_of[(g, start, half)]
             return product(h_codes, h_scales, rt, codes, scales, first, cols)
 
-        for i in range(10):
+        for i in range(9):
             open_by(i)
         gates_done = ups_done = 0
-        i = 11
+        i = 10
         while i <= len(units) or ups_done < len(open_tiles[1]):
             gates = open_tiles[0][gates_done : gates_done + TILES_A_STEP]
             ups = open_tiles[1][ups_done : min(ups_done + TILES_A_STEP, gates_done)]

@@ -25,8 +25,8 @@ UNIT = FF // 2
 QUANT_COLS = 1024
 RUN = 8
 PE_COLS = 256
-O_VECTOR_COLS, VECTOR_COLS = 512, 512
-FIRST_GROUP_VECTOR_COLS = 576
+VECTOR_COLS = 512
+GPSIMD_COLS, GPSIMD_RELIEF = 128, 80
 RAW_BUFS = 5
 X_MID_STEP = 12
 RESULT_BUFS = 5
@@ -130,22 +130,34 @@ def tile_twomodelblockrouted_pb_kernel(tc, attn, x, W_o, W_gu, ln2, x_mid_out, h
                     stop=True,
                 )
 
+        def regrouping(i, first, last):
+            to = grouped_of[i][:, first:last, :].rearrange("p (c i) t -> p c t i", i=RUN)
+            return to, raw_of[i][:, :, first:last].rearrange("p t (c i) -> p c t i", i=RUN)
+
+        def gpsimd_regroup(i):
+            if i >= len(units):
+                return
+            grouped_of[i] = grouped_pool.tile([P, UNIT, PACK], BF16, name="grouped", align_bytes=64)
+            first = VECTOR_COLS - GPSIMD_RELIEF
+            to, source = regrouping(i, first, first + GPSIMD_COLS)
+            nc.gpsimd.tensor_scalar(out=to, in0=source, scalar1=1.0, scalar2=0.0, op0=ALU.mult, op1=ALU.add)
+
         def step(i):
             if i >= len(units):
                 return
             width = units[i][3]
             direct = width - tensor_cols(i)
-            kind, g, begin = units[i][:3]
-            vector = O_VECTOR_COLS if kind == "o" else FIRST_GROUP_VECTOR_COLS if (g, begin) == groups[0] else VECTOR_COLS
-            grouped = grouped_pool.tile([P, UNIT, PACK], BF16, name="grouped", align_bytes=64)
+            if i in grouped_of:
+                vector, scalar = VECTOR_COLS - GPSIMD_RELIEF, VECTOR_COLS - GPSIMD_RELIEF + GPSIMD_COLS
+            else:
+                vector = scalar = VECTOR_COLS
+                grouped_of[i] = grouped_pool.tile([P, UNIT, PACK], BF16, name="grouped", align_bytes=64)
             if direct < width:
-                nc.scalar.copy(out=grouped[:, direct:width, :], in_=bank_of[i][:])
-            for copy, first, last in ((nc.vector.tensor_copy, 0, vector), (nc.scalar.copy, vector, direct)):
-                copy(
-                    out=grouped[:, first:last, :].rearrange("p (c i) t -> p c t i", i=RUN),
-                    in_=raw_of[i][:, :, first:last].rearrange("p t (c i) -> p c t i", i=RUN),
-                )
-            grouped_of[i] = grouped
+                nc.scalar.copy(out=grouped_of[i][:, direct:width, :], in_=bank_of[i][:])
+            to, source = regrouping(i, 0, vector)
+            nc.vector.tensor_copy(out=to, in_=source)
+            to, source = regrouping(i, scalar, direct)
+            nc.scalar.copy(out=to, in_=source)
             load(i + RAW_BUFS)
 
         def quantise(i):
@@ -284,9 +296,9 @@ def tile_twomodelblockrouted_pb_kernel(tc, attn, x, W_o, W_gu, ln2, x_mid_out, h
         nc.gpsimd.tensor_tensor(out=rstd[:], in0=variance[:], in1=minus_half[:], op=ALU.pow)
         tensor_regroup(6)
         step(6)
-        quantise(5)
         gains = [spread_gains(g) for g in range(MODELS)]
         h_rows = [normalise(rt, gains[0]) for rt in (0, 1)]
+        quantise(5)
         tensor_regroup(7)
         step(7)
         h_turned = [turn(h[:].bitcast(F32), acc_pool, "acc") for h in h_rows]
@@ -340,6 +352,8 @@ def tile_twomodelblockrouted_pb_kernel(tc, attn, x, W_o, W_gu, ln2, x_mid_out, h
             quantise(i - 1)
             if i - 1 < len(units):
                 open_by(i - 1)
+            if ups:
+                gpsimd_regroup(i + 1)
             for (g, start, rt, first, cols), acc in zip(ups, up_accs):
                 result = results[(start, rt)]
                 piece = result[:, first : first + cols]

@@ -134,6 +134,10 @@ def tile_twomodelblockrouted_pb_kernel(tc, attn, x, W_o, W_gu, ln2, x_mid_out, h
             to = grouped_of[i][:, first:last, :].rearrange("p (c i) t -> p c t i", i=RUN)
             return to, raw_of[i][:, :, first:last].rearrange("p t (c i) -> p c t i", i=RUN)
 
+        def pairwise(i, first, last):
+            to = grouped_of[i][:, first:last, :].rearrange("p (c i) (u e) -> p c u i e", i=RUN, e=2)
+            return to, raw_of[i][:, :, first:last].rearrange("p (u e) (c i) -> p c u i e", i=RUN, e=2)
+
         def gpsimd_regroup(i):
             if i >= len(units):
                 return
@@ -154,7 +158,7 @@ def tile_twomodelblockrouted_pb_kernel(tc, attn, x, W_o, W_gu, ln2, x_mid_out, h
                 grouped_of[i] = grouped_pool.tile([P, UNIT, PACK], BF16, name="grouped", align_bytes=64)
             if direct < width:
                 nc.scalar.copy(out=grouped_of[i][:, direct:width, :], in_=bank_of[i][:])
-            to, source = regrouping(i, 0, vector)
+            to, source = pairwise(i, 0, vector)
             nc.vector.tensor_copy(out=to, in_=source)
             to, source = regrouping(i, scalar, direct)
             nc.scalar.copy(out=to, in_=source)

from contextlib import ExitStack

import concourse.mybir as mybir
from concourse.masks import make_identity

F32 = mybir.dt.float32
BF16 = mybir.dt.bfloat16
I32 = mybir.dt.int32
U32 = mybir.dt.uint32
U8 = mybir.dt.uint8
FP8X4 = mybir.dt.float8_e4m3fn_x4
ACT = mybir.ActivationFunctionType
ALU = mybir.AluOpType

P = 128
PACK = 4
K_PASS = P * PACK
ROWS, SPLIT_ROW, H, FF = 512, 384, 1024, 2560
EPS = 1.1920929e-07
MODELS = 2
PASSES = H // K_PASS
ROW_TILES = ROWS // P
N_TILE = 512
UNIT = FF // 2
QUANT_COLS = 1024
RUN = 8
PE_COLS = 256
VECTOR_COLS = 512
GPSIMD_COLS, GPSIMD_RELIEF = 128, 80
RAW_BUFS = 5
X_MID_STEP = 12
RESULT_BUFS = 5
TILES_A_STEP = 3

FLOPS = 2 * ROWS * H * H + 2 * ROWS * H * 2 * FF


ROW_TILES_0 = SPLIT_ROW // P


def model_of(row_tile):
    return 0 if row_tile < ROW_TILES_0 else 1


def by_row_tile(rows):
    return (
        rows[:SPLIT_ROW, :].rearrange("(p rt) n -> p rt n", rt=ROW_TILES_0),
        rows[SPLIT_ROW:, :].rearrange("(p rt) n -> p rt n", rt=1),
    )


def cut(width, piece):
    return [(first, min(piece, width - first)) for first in range(0, width, piece)]


def tile_twomodelblockrouted_pb_kernel(tc, attn, x, W_o, W_gu, ln2, x_mid_out, h_mlp_out):
    nc = tc.nc
    with ExitStack() as stack:
        keep = stack.enter_context(tc.tile_pool(name="keep", bufs=1))
        raw_pool = stack.enter_context(tc.tile_pool(name="raw", bufs=RAW_BUFS))
        grouped_pool = stack.enter_context(tc.tile_pool(name="grouped", bufs=3))
        gate_pool = stack.enter_context(tc.tile_pool(name="gate_codes", bufs=3))
        up_pool = stack.enter_context(tc.tile_pool(name="up_codes", bufs=2))
        work = stack.enter_context(tc.tile_pool(name="work", bufs=2))
        rows_pool = stack.enter_context(tc.tile_pool(name="rows", bufs=ROW_TILES))
        result_pool = stack.enter_context(tc.tile_pool(name="result", bufs=RESULT_BUFS))
        bank_pool = stack.enter_context(tc.psum_pool(name="bank", bufs=2))
        acc_pool = stack.enter_context(tc.psum_pool(name="acc", bufs=6))
        stack.enter_context(tc.manual_schedule())

        gain_row = result_pool.tile([P, MODELS * H], BF16, name="result")
        nc.gpsimd.memset(gain_row[:].bitcast(I32), 0)
        ident_f32 = keep.tile([P, P], F32)
        make_identity(nc, ident_f32[:])
        ident_bf16 = keep.tile([P, P], BF16)
        make_identity(nc, ident_bf16[:])
        minus_half = keep.tile([P, ROW_TILES], F32)
        nc.vector.memset(minus_half[:], -0.5)
        warm = keep.tile([P, 1], F32)
        nc.scalar.activation(out=warm[:], in_=minus_half[:, 0:1], func=ACT.Silu)
        ones = keep.tile([P, P], BF16)
        nc.vector.memset(ones[:], 1.0)

        x_mid = keep.tile([P, ROW_TILES, H], F32)
        attn_codes = keep.tile([P, ROW_TILES, PASSES * P], U32, align_bytes=64)
        attn_scales = keep.tile([P, ROW_TILES, PASSES * P], U8, align_bytes=64)
        h_codes = keep.tile([P, ROW_TILES, PASSES * P], U32, align_bytes=64)
        h_scales = keep.tile([P, ROW_TILES, PASSES * P], U8, align_bytes=64)
        sum_sq = keep.tile([P, ROW_TILES], F32)
        variance = keep.tile([P, ROW_TILES], F32)
        rstd = keep.tile([P, ROW_TILES], F32)

        wo_codes = keep.tile([P, MODELS, PASSES, H], U32, align_bytes=64)
        wo_scales = keep.tile([P, MODELS, PASSES, H], U8, align_bytes=64)
        attn_sb = gate_pool.tile([P, ROW_TILES, H], BF16, name="codes", align_bytes=64)
        x_sb = up_pool.tile([P, ROW_TILES, H], BF16, name="codes", align_bytes=64)

        units = [("o", g, 0, H, 0, c) for g in range(MODELS) for c in range(PASSES)]
        groups = [(g, start) for g in range(MODELS) for start in range(0, FF, UNIT)]
        units.extend([("gu", g, start, UNIT, half, c) for g, start in groups for half in range(2) for c in range(PASSES)])
        raw_of, bank_of, grouped_of, codes_of = {}, {}, {}, {}

        def load(i):
            if i >= len(units):
                return
            kind, g, start, width, half, c = units[i]
            buffer = raw_pool.tile([P, PACK * UNIT], BF16, name="raw")
            raw_of[i] = buffer[:, : PACK * width].rearrange("p (t n) -> p t n", t=PACK)
            k_rows = slice(c * K_PASS, (c + 1) * K_PASS)
            if kind == "o":
                rows = W_o[g, k_rows, :]
            else:
                rows = W_gu[g, k_rows, half * FF + start : half * FF + start + width]
            nc.sync.dma_start(out=raw_of[i], in_=rows.rearrange("(p t) n -> p t n", t=PACK))

        def tensor_cols(i):
            return PE_COLS if i < len(units) and units[i][0] == "gu" else 0

        def tensor_regroup(i):
            if tensor_cols(i) == 0:
                return
            direct = units[i][3] - PE_COLS
            bank_of[i] = bank_pool.tile([P, PE_COLS, PACK], BF16, name="bank")
            for first in range(0, PE_COLS, P):
                nc.tensor.matmul(
                    out=bank_of[i][:, first : first + P, :].rearrange("p n t -> p t n"),
                    lhsT=ident_bf16[:],
                    rhs=raw_of[i][:, :, direct + first : direct + first + P],
                    start=True,
                    stop=True,
                )

        def regrouping(i, first, last):
            to = grouped_of[i][:, first:last, :].rearrange("p (c i) t -> p c t i", i=RUN)
            return to, raw_of[i][:, :, first:last].rearrange("p t (c i) -> p c t i", i=RUN)

        def pairwise(i, first, last):
            to = grouped_of[i][:, first:last, :].rearrange("p (c i) (u e) -> p c u i e", i=RUN, e=2)
            return to, raw_of[i][:, :, first:last].rearrange("p (u e) (c i) -> p c u i e", i=RUN, e=2)

        def gpsimd_regroup(i):
            if i >= len(units):
                return
            grouped_of[i] = grouped_pool.tile([P, UNIT, PACK], BF16, name="grouped", align_bytes=64)
            first = VECTOR_COLS - GPSIMD_RELIEF
            to, source = regrouping(i, first, first + GPSIMD_COLS)
            nc.gpsimd.tensor_scalar(out=to, in0=source, scalar1=1.0, scalar2=0.0, op0=ALU.mult, op1=ALU.add)

        def step(i):
            if i >= len(units):
                return
            width = units[i][3]
            direct = width - tensor_cols(i)
            if i in grouped_of:
                vector, scalar = VECTOR_COLS - GPSIMD_RELIEF, VECTOR_COLS - GPSIMD_RELIEF + GPSIMD_COLS
            else:
                vector = scalar = VECTOR_COLS
                grouped_of[i] = grouped_pool.tile([P, UNIT, PACK], BF16, name="grouped", align_bytes=64)
            if direct < width:
                nc.scalar.copy(out=grouped_of[i][:, direct:width, :], in_=bank_of[i][:])
            to, source = pairwise(i, 0, vector)
            nc.vector.tensor_copy(out=to, in_=source)
            to, source = regrouping(i, scalar, direct)
            nc.scalar.copy(out=to, in_=source)
            load(i + RAW_BUFS)

        def quantise(i):
            if i >= len(units):
                return
            kind, g, start, width, half, c = units[i]
            if kind == "o":
                codes, scales = wo_codes[:, g, c, :], wo_scales[:, g, c, :]
            else:
                if c == 0:
                    pool = (gate_pool, up_pool)[half]
                    half_codes = pool.tile([P, PASSES, UNIT], U32, name="codes", align_bytes=64)
                    half_scales = pool.tile([P, PASSES, UNIT], U8, name="scales", align_bytes=64)
                    codes_of[(g, start, half)] = (half_codes, half_scales)
                codes, scales = [plane[:, c, :] for plane in codes_of[(g, start, half)]]
            for first, cols in cut(width, QUANT_COLS if i + 1 < len(units) else N_TILE):
                nc.vector.quantize_mx(
                    out=codes[:, first : first + cols].bitcast(FP8X4),
                    scales=scales[:, first : first + cols],
                    in_=grouped_of[i][:, first : first + cols, :].rearrange("p n t -> p (n t)"),
                )

        def quantise_rows(grouped, codes, scales, rt):
            nc.vector.quantize_mx(out=codes[:, rt, :].bitcast(FP8X4), scales=scales[:, rt, :], in_=grouped[:])

        def product(rows_codes, rows_scales, rt, w_codes, w_scales, first, width):
            acc = acc_pool.tile([P, N_TILE], F32, name="acc")
            for c in range(PASSES):
                nc.tensor.matmul_mx(
                    out=acc[:, :width],
                    lhsT=rows_codes[:, rt, c * P : (c + 1) * P].bitcast(FP8X4),
                    lhsT_scale=rows_scales[:, rt, c * P : (c + 1) * P],
                    rhs=w_codes[:, c, first : first + width].bitcast(FP8X4),
                    rhs_scale=w_scales[:, c, first : first + width],
                    start=(c == 0),
                    stop=(c == PASSES - 1),
                )
            return acc

        def turn(words, pool, tag):
            turned = pool.tile([P, PASSES * 2, P], F32, name=tag)
            for c in range(PASSES):
                for u in range(2):
                    pairs = words[:, 2 * P * c + u : 2 * P * (c + 1) : 2]
                    nc.tensor.transpose(turned[:, 2 * c + u, :], pairs, ident_f32[:])
            return turned

        def group_rows(turned):
            grouped = rows_pool.tile([P, PASSES * P * PACK], BF16, name="rows_grouped", align_bytes=64)
            nc.scalar.copy(
                out=grouped[:].bitcast(F32).rearrange("p (c r u) -> p c r u", c=PASSES, u=2),
                in_=turned[:].rearrange("p (c u) r -> p c r u", u=2),
            )
            return grouped

        def first_product(rt):
            g = model_of(rt)
            return [
                product(attn_codes, attn_scales, rt, wo_codes[:, g], wo_scales[:, g], first, N_TILE)
                for first in range(0, H, N_TILE)
            ]

        def add_x(rt, accs):
            for n, acc in enumerate(accs):
                cols = slice(n * N_TILE, (n + 1) * N_TILE)
                nc.vector.tensor_tensor(out=x_mid[:, rt, cols], in0=acc[:], in1=x_sb[:, rt, cols], op=ALU.add)

        def square(rt):
            squares = work.tile([P, H], BF16, name="squares")
            nc.scalar.activation(out=squares[:], in_=x_mid[:, rt, :], func=ACT.Square, accum_out=sum_sq[:, rt : rt + 1])

        def spread_gains(g):
            gains = acc_pool.tile([P, H], BF16, name="acc")
            for first in range(0, H, N_TILE):
                row = gain_row[:, g * H + first : g * H + first + N_TILE]
                nc.tensor.matmul(out=gains[:, first : first + N_TILE], lhsT=ones[:], rhs=row, start=True, stop=True)
            return gains

        def normalise(rt, gains):
            h = work.tile([P, H], BF16, name="h")
            nc.vector.scalar_tensor_tensor(
                out=h[:],
                in0=x_mid[:, rt, :],
                scalar=rstd[:, rt : rt + 1],
                in1=gains[:],
                op0=ALU.mult,
                op1=ALU.mult,
            )
            return h

        def load_rows(tile, rows):
            first, last = by_row_tile(rows)
            nc.sync.dma_start(out=tile[:, :ROW_TILES_0, :], in_=first)
            nc.sync.dma_start(out=tile[:, ROW_TILES_0:, :], in_=last)

        def rows_of(out, rt):
            first, last = by_row_tile(out)
            return first[:, rt, :] if rt < ROW_TILES_0 else last[:, 0, :]

        load(0)
        nc.sync.dma_start(out=gain_row[0:1, :], in_=ln2.rearrange("(o g) k -> o (g k)", o=1))
        load(1)
        load(2)
        load_rows(attn_sb, attn)
        load(3)
        load_rows(x_sb, x)
        load(4)

        step(0)
        quantise(0)
        step(1)
        quantise(1)
        step(2)
        attn_grouped = [group_rows(turn(attn_sb[:, rt, :].bitcast(F32), bank_pool, "bank")) for rt in range(ROW_TILES)]
        quantise(2)
        for rt in range(ROW_TILES):
            quantise_rows(attn_grouped[rt], attn_codes, attn_scales, rt)
        step(3)
        accs = [first_product(rt) for rt in (0, 1, 2)]
        add_x(0, accs[0])
        square(0)
        quantise(3)
        add_x(1, accs[1])
        square(1)
        add_x(2, accs[2])
        accs.append(first_product(3))
        tensor_regroup(4)
        step(4)
        square(2)
        add_x(3, accs[3])
        square(3)
        tensor_regroup(5)
        step(5)
        quantise(4)
        nc.gpsimd.tensor_scalar(out=variance[:], in0=sum_sq[:], scalar1=1.0 / H, scalar2=EPS, op0=ALU.mult, op1=ALU.add)
        nc.gpsimd.tensor_tensor(out=rstd[:], in0=variance[:], in1=minus_half[:], op=ALU.pow)
        tensor_regroup(6)
        step(6)
        gains = [spread_gains(g) for g in range(MODELS)]
        h_rows = [normalise(rt, gains[0]) for rt in (0, 1)]
        quantise(5)
        tensor_regroup(7)
        step(7)
        h_turned = [turn(h[:].bitcast(F32), acc_pool, "acc") for h in h_rows]
        quantise(6)
        h_grouped = [group_rows(turned) for turned in h_turned]
        h_rows = [normalise(2, gains[0]), normalise(3, gains[1])]
        tensor_regroup(8)
        step(8)
        h_turned = [turn(h[:].bitcast(F32), acc_pool, "acc") for h in h_rows]
        quantise(7)
        h_grouped.extend([group_rows(turned) for turned in h_turned])
        quantise_rows(h_grouped[0], h_codes, h_scales, 0)
        quantise_rows(h_grouped[1], h_codes, h_scales, 1)
        tensor_regroup(9)
        step(9)
        quantise(8)
        quantise_rows(h_grouped[2], h_codes, h_scales, 2)
        quantise_rows(h_grouped[3], h_codes, h_scales, 3)
        tensor_regroup(10)

        open_tiles = ([], [])
        results = {}

        def open_by(i):
            kind, g, start, width, half, c = units[i]
            if kind == "gu" and c == PASSES - 1:
                row_tiles = [rt for rt in range(ROW_TILES) if model_of(rt) == g]
                open_tiles[half].extend([(g, start, rt) + piece for rt in row_tiles for piece in cut(UNIT, N_TILE)])

        def second_product(half, g, start, rt, first, cols):
            codes, scales = codes_of[(g, start, half)]
            return product(h_codes, h_scales, rt, codes, scales, first, cols)

        for i in range(9):
            open_by(i)
        gates_done = ups_done = 0
        i = 10
        while i <= len(units) or ups_done < len(open_tiles[1]):
            gates = open_tiles[0][gates_done : gates_done + TILES_A_STEP]
            ups = open_tiles[1][ups_done : min(ups_done + TILES_A_STEP, gates_done)]
            gate_accs = [second_product(0, *tile) for tile in gates]
            up_accs = [second_product(1, *tile) for tile in ups]
            tensor_regroup(i + 1)
            step(i)
            for (g, start, rt, first, cols), acc in zip(gates, gate_accs):
                if first == 0:
                    results[(start, rt)] = result_pool.tile([P, UNIT], F32, name="result")
                nc.scalar.activation(
                    out=results[(start, rt)][:, first : first + cols], in_=acc[:, :cols], func=ACT.Silu
                )
            quantise(i - 1)
            if i - 1 < len(units):
                open_by(i - 1)
            if ups:
                gpsimd_regroup(i + 1)
            for (g, start, rt, first, cols), acc in zip(ups, up_accs):
                result = results[(start, rt)]
                piece = result[:, first : first + cols]
                nc.vector.tensor_tensor(out=piece, in0=acc[:, :cols], in1=piece, op=ALU.mult)
                if (g, start) == groups[-1]:
                    nc.sync.dma_start(out=rows_of(h_mlp_out, rt)[:, start + first : start + first + cols], in_=piece)
                elif first + cols == UNIT:
                    nc.sync.dma_start(out=rows_of(h_mlp_out, rt)[:, start : start + UNIT], in_=result[:])
            if i == X_MID_STEP:
                first, last = by_row_tile(x_mid_out)
                nc.sync.dma_start(out=first, in_=x_mid[:, :ROW_TILES_0, :])
                nc.sync.dma_start(out=last, in_=x_mid[:, ROW_TILES_0:, :])
            gates_done += len(gates)
            ups_done += len(ups)
            i += 1
